import numpy as np
import ml_dtypes

BF16 = ml_dtypes.bfloat16


def bf(x):
    return np.asarray(x, np.float32).astype(BF16)


def f32(x):
    return np.asarray(x, np.float32)


def f64(x):
    return np.asarray(x).astype(np.float64)


def striped(idx):
    return np.tile(idx.reshape(-1, 16).T, (8, 1))


D, C, S, N = 256, 512, 2048, 512


def sigmoid(v):
    return 1.0 / (1.0 + np.exp(-v))


def setup_inputs():
    return {"base": f32(np.random.standard_normal((C, S))), "x": bf(np.random.standard_normal((D, N))), "carry": f32(np.random.standard_normal((C, N))), "w_u": bf(np.random.standard_normal((D, C)) / np.sqrt(D)), "b_u": f32(0.5 * np.random.standard_normal((C, 1))), "w_c": bf(np.random.standard_normal((D, C)) / np.sqrt(D)), "b_c": f32(0.5 * np.random.standard_normal((C, 1))), "offs": striped(np.random.permutation(S)[:N])}


def reference(base, x, carry, w_u, b_u, w_c, b_c, offs):
    idx = offs[:16].T.reshape(-1)
    u = sigmoid(f64(w_u).T @ f64(x) + f64(b_u))
    cand = np.tanh(f64(w_c).T @ f64(x) + f64(b_c))
    out = f64(base).copy()
    out[:, idx] = (1.0 - u) * cand + u * f64(carry)
    return out

@@ -1,0 +1,71 @@
+import concourse.mybir as mybir
+
+P = 128
+D, C, S, N = 256, 512, 2048, 512
+D_BLOCKS = D // P
+C_BLOCKS = C // P
+
+FLOPS = 2 * 2 * D * C * N
+
+F32, BF16, U16 = mybir.dt.float32, mybir.dt.bfloat16, mybir.dt.uint16
+ADD, SUBTRACT, MULT = mybir.AluOpType.add, mybir.AluOpType.subtract, mybir.AluOpType.mult
+SIGMOID, TANH = mybir.ActivationFunctionType.Sigmoid, mybir.ActivationFunctionType.Tanh
+
+
+def tile_loraexplicitgrucell_kernel(tc, base, x, carry, w_u, b_u, w_c, b_c, offs, out):
+    nc = tc.nc
+    with (
+        tc.tile_pool(name="held", bufs=1) as held,
+        tc.tile_pool(name="work", bufs=2) as work,
+        tc.psum_pool(name="psum", bufs=2) as psum,
+    ):
+        offsets = held.tile([P, N // 16], U16, name="offsets")
+        nc.sync.dma_start(offsets[:], offs)
+
+        x_sb = held.tile([P, D_BLOCKS, N], BF16, name="x_sb")
+        nc.sync.dma_start(x_sb[:], x.rearrange("(k p) n -> p k n", p=P))
+        w_c_sb = held.tile([P, D_BLOCKS, C], BF16, name="w_c_sb")
+        nc.sync.dma_start(w_c_sb[:], w_c.rearrange("(k p) c -> p k c", p=P))
+        w_u_sb = held.tile([P, D_BLOCKS, C], BF16, name="w_u_sb")
+        nc.sync.dma_start(w_u_sb[:], w_u.rearrange("(k p) c -> p k c", p=P))
+
+        b_c_sb = held.tile([P, C_BLOCKS], F32, name="b_c_sb")
+        b_u_sb = held.tile([P, C_BLOCKS], F32, name="b_u_sb")
+        with nc.allow_non_contiguous_dma(reason="512 biases, one to a partition"):
+            nc.sync.dma_start(b_c_sb[:], b_c.rearrange("(b p) o -> p (b o)", p=P))
+            nc.sync.dma_start(b_u_sb[:], b_u.rearrange("(b p) o -> p (b o)", p=P))
+
+        carries = []
+        windows = []
+        for b in range(C_BLOCKS):
+            rows = slice(b * P, (b + 1) * P)
+            carry_sb = held.tile([P, N], F32, name=f"carry{b}")
+            nc.sync.dma_start(carry_sb[:], carry[rows, :])
+            carries.append(carry_sb)
+            window = held.tile([P, S], F32, name=f"window{b}")
+            nc.sync.dma_start(window[:], base[rows, :])
+            windows.append(window)
+
+        for b in range(C_BLOCKS):
+            rows = slice(b * P, (b + 1) * P)
+
+            z_c = psum.tile([P, N], F32, name="z_c")
+            z_u = psum.tile([P, N], F32, name="z_u")
+            for z, w_sb in ((z_c, w_c_sb), (z_u, w_u_sb)):
+                for k in range(D_BLOCKS):
+                    nc.tensor.matmul(
+                        z[:], w_sb[:, k, rows], x_sb[:, k, :], start=(k == 0), stop=(k == D_BLOCKS - 1)
+                    )
+
+            cand = work.tile([P, N], F32, name="cand")
+            nc.scalar.activation(cand[:], z_c[:], TANH, bias=b_c_sb[:, b : b + 1])
+            u = work.tile([P, N], F32, name="u")
+            nc.scalar.activation(u[:], z_u[:], SIGMOID, bias=b_u_sb[:, b : b + 1])
+
+            diff = work.tile([P, N], F32, name="diff")
+            nc.vector.tensor_tensor(diff[:], carries[b][:], cand[:], SUBTRACT)
+            gated = work.tile([P, N], F32, name="gated")
+            nc.vector.tensor_tensor(gated[:], u[:], diff[:], MULT)
+            nc.vector.tensor_tensor(windows[b][:].indirect(offsets[:]), gated[:], cand[:], ADD)
+
+            nc.sync.dma_start(out[rows, :], windows[b][:])

@@ -14,47 +14,53 @@ SIGMOID, TANH = mybir.ActivationFunctionType.Sigmoid, mybir.ActivationFunctionTy
 
 def tile_loraexplicitgrucell_kernel(tc, base, x, carry, w_u, b_u, w_c, b_c, offs, out):
     nc = tc.nc
+    base_blocks = base.rearrange("(p b) s -> b p s", b=C_BLOCKS)
+    carry_blocks = carry.rearrange("(p b) n -> b p n", b=C_BLOCKS)
+    out_blocks = out.rearrange("(p b) s -> b p s", b=C_BLOCKS)
+
     with (
         tc.tile_pool(name="held", bufs=1) as held,
         tc.tile_pool(name="work", bufs=2) as work,
         tc.psum_pool(name="psum", bufs=2) as psum,
     ):
+        warm = held.tile([P, 1], F32, name="warm")
+        nc.gpsimd.memset(warm[:], 0.0)
+        nc.scalar.activation(warm[:], warm[:], SIGMOID)
+
         offsets = held.tile([P, N // 16], U16, name="offsets")
         nc.sync.dma_start(offsets[:], offs)
 
         x_sb = held.tile([P, D_BLOCKS, N], BF16, name="x_sb")
-        nc.sync.dma_start(x_sb[:], x.rearrange("(k p) n -> p k n", p=P))
+        nc.sync.dma_start(x_sb[:], x.rearrange("(p k) n -> p k n", k=D_BLOCKS))
         w_c_sb = held.tile([P, D_BLOCKS, C], BF16, name="w_c_sb")
-        nc.sync.dma_start(w_c_sb[:], w_c.rearrange("(k p) c -> p k c", p=P))
-        w_u_sb = held.tile([P, D_BLOCKS, C], BF16, name="w_u_sb")
-        nc.sync.dma_start(w_u_sb[:], w_u.rearrange("(k p) c -> p k c", p=P))
-
+        nc.sync.dma_start(w_c_sb[:], w_c.rearrange("(p k) c -> p k c", k=D_BLOCKS))
         b_c_sb = held.tile([P, C_BLOCKS], F32, name="b_c_sb")
+        nc.sync.dma_start(b_c_sb[:], b_c.rearrange("(p b) o -> p (b o)", b=C_BLOCKS))
+        w_u_sb = held.tile([P, D_BLOCKS, C], BF16, name="w_u_sb")
+        nc.sync.dma_start(w_u_sb[:], w_u.rearrange("(p k) c -> p k c", k=D_BLOCKS))
         b_u_sb = held.tile([P, C_BLOCKS], F32, name="b_u_sb")
-        with nc.allow_non_contiguous_dma(reason="512 biases, one to a partition"):
-            nc.sync.dma_start(b_c_sb[:], b_c.rearrange("(b p) o -> p (b o)", p=P))
-            nc.sync.dma_start(b_u_sb[:], b_u.rearrange("(b p) o -> p (b o)", p=P))
+        nc.sync.dma_start(b_u_sb[:], b_u.rearrange("(p b) o -> p (b o)", b=C_BLOCKS))
 
         carries = []
         windows = []
         for b in range(C_BLOCKS):
-            rows = slice(b * P, (b + 1) * P)
             carry_sb = held.tile([P, N], F32, name=f"carry{b}")
-            nc.sync.dma_start(carry_sb[:], carry[rows, :])
+            nc.sync.dma_start(carry_sb[:], carry_blocks[b])
             carries.append(carry_sb)
             window = held.tile([P, S], F32, name=f"window{b}")
-            nc.sync.dma_start(window[:], base[rows, :])
+            nc.sync.dma_start(window[:], base_blocks[b])
             windows.append(window)
 
-        for b in range(C_BLOCKS):
-            rows = slice(b * P, (b + 1) * P)
+        w_c_blocks = w_c_sb[:].rearrange("p k (m b) -> p k b m", b=C_BLOCKS)
+        w_u_blocks = w_u_sb[:].rearrange("p k (m b) -> p k b m", b=C_BLOCKS)
 
+        for b in range(C_BLOCKS):
             z_c = psum.tile([P, N], F32, name="z_c")
             z_u = psum.tile([P, N], F32, name="z_u")
-            for z, w_sb in ((z_c, w_c_sb), (z_u, w_u_sb)):
+            for z, w_blocks in ((z_c, w_c_blocks), (z_u, w_u_blocks)):
                 for k in range(D_BLOCKS):
                     nc.tensor.matmul(
-                        z[:], w_sb[:, k, rows], x_sb[:, k, :], start=(k == 0), stop=(k == D_BLOCKS - 1)
+                        z[:], w_blocks[:, k, b, :], x_sb[:, k, :], start=(k == 0), stop=(k == D_BLOCKS - 1)
                     )
 
             cand = work.tile([P, N], F32, name="cand")
@@ -63,9 +69,9 @@ def tile_loraexplicitgrucell_kernel(tc, base, x, carry, w_u, b_u, w_c, b_c, offs
             nc.scalar.activation(u[:], z_u[:], SIGMOID, bias=b_u_sb[:, b : b + 1])
 
             diff = work.tile([P, N], F32, name="diff")
-            nc.vector.tensor_tensor(diff[:], carries[b][:], cand[:], SUBTRACT)
+            nc.gpsimd.tensor_tensor(diff[:], carries[b][:], cand[:], SUBTRACT)
             gated = work.tile([P, N], F32, name="gated")
-            nc.vector.tensor_tensor(gated[:], u[:], diff[:], MULT)
+            nc.gpsimd.tensor_tensor(gated[:], u[:], diff[:], MULT)
             nc.vector.tensor_tensor(windows[b][:].indirect(offsets[:]), gated[:], cand[:], ADD)
 
-            nc.sync.dma_start(out[rows, :], windows[b][:])
+            nc.sync.dma_start(out_blocks[b], windows[b][:])

@@ -20,15 +20,11 @@ def tile_loraexplicitgrucell_kernel(tc, base, x, carry, w_u, b_u, w_c, b_c, offs
 
     with (
         tc.tile_pool(name="held", bufs=1) as held,
-        tc.tile_pool(name="work", bufs=2) as work,
         tc.psum_pool(name="psum", bufs=2) as psum,
     ):
         warm = held.tile([P, 1], F32, name="warm")
         nc.gpsimd.memset(warm[:], 0.0)
         nc.scalar.activation(warm[:], warm[:], SIGMOID)
-
-        offsets = held.tile([P, N // 16], U16, name="offsets")
-        nc.sync.dma_start(offsets[:], offs)
 
         x_sb = held.tile([P, D_BLOCKS, N], BF16, name="x_sb")
         nc.sync.dma_start(x_sb[:], x.rearrange("(p k) n -> p k n", k=D_BLOCKS))
@@ -40,6 +36,8 @@ def tile_loraexplicitgrucell_kernel(tc, base, x, carry, w_u, b_u, w_c, b_c, offs
         nc.sync.dma_start(w_u_sb[:], w_u.rearrange("(p k) c -> p k c", k=D_BLOCKS))
         b_u_sb = held.tile([P, C_BLOCKS], F32, name="b_u_sb")
         nc.sync.dma_start(b_u_sb[:], b_u.rearrange("(p b) o -> p (b o)", b=C_BLOCKS))
+        offsets = held.tile([P, N // 16], U16, name="offsets")
+        nc.sync.dma_start(offsets[:], offs)
 
         carries = []
         windows = []
@@ -54,6 +52,11 @@ def tile_loraexplicitgrucell_kernel(tc, base, x, carry, w_u, b_u, w_c, b_c, offs
         w_c_blocks = w_c_sb[:].rearrange("p k (m b) -> p k b m", b=C_BLOCKS)
         w_u_blocks = w_u_sb[:].rearrange("p k (m b) -> p k b m", b=C_BLOCKS)
 
+        cands = [held.tile([P, N], F32, name=f"cand{b}") for b in range(C_BLOCKS)]
+        us = [held.tile([P, N], F32, name=f"u{b}") for b in range(C_BLOCKS)]
+        diffs = [held.tile([P, N], F32, name=f"diff{b}") for b in range(C_BLOCKS)]
+        gateds = [held.tile([P, N], F32, name=f"gated{b}") for b in range(C_BLOCKS)]
+
         for b in range(C_BLOCKS):
             z_c = psum.tile([P, N], F32, name="z_c")
             z_u = psum.tile([P, N], F32, name="z_u")
@@ -62,16 +65,13 @@ def tile_loraexplicitgrucell_kernel(tc, base, x, carry, w_u, b_u, w_c, b_c, offs
                     nc.tensor.matmul(
                         z[:], w_blocks[:, k, b, :], x_sb[:, k, :], start=(k == 0), stop=(k == D_BLOCKS - 1)
                     )
+            nc.scalar.activation(cands[b][:], z_c[:], TANH, bias=b_c_sb[:, b : b + 1])
+            nc.scalar.activation(us[b][:], z_u[:], SIGMOID, bias=b_u_sb[:, b : b + 1])
 
-            cand = work.tile([P, N], F32, name="cand")
-            nc.scalar.activation(cand[:], z_c[:], TANH, bias=b_c_sb[:, b : b + 1])
-            u = work.tile([P, N], F32, name="u")
-            nc.scalar.activation(u[:], z_u[:], SIGMOID, bias=b_u_sb[:, b : b + 1])
-
-            diff = work.tile([P, N], F32, name="diff")
-            nc.gpsimd.tensor_tensor(diff[:], carries[b][:], cand[:], SUBTRACT)
-            gated = work.tile([P, N], F32, name="gated")
-            nc.gpsimd.tensor_tensor(gated[:], u[:], diff[:], MULT)
-            nc.vector.tensor_tensor(windows[b][:].indirect(offsets[:]), gated[:], cand[:], ADD)
-
+        nc.vector.tensor_tensor(diffs[0][:], carries[0][:], cands[0][:], SUBTRACT)
+        for b in range(C_BLOCKS):
+            nc.vector.tensor_tensor(gateds[b][:], us[b][:], diffs[b][:], MULT)
+            if b + 1 < C_BLOCKS:
+                nc.vector.tensor_tensor(diffs[b + 1][:], carries[b + 1][:], cands[b + 1][:], SUBTRACT)
+            nc.vector.tensor_tensor(windows[b][:].indirect(offsets[:]), gateds[b][:], cands[b][:], ADD)
             nc.sync.dma_start(out_blocks[b], windows[b][:])

@@ -1,9 +1,12 @@
 import concourse.mybir as mybir
+from concourse.masks import make_identity
 
 P = 128
 D, C, S, N = 256, 512, 2048, 512
 D_BLOCKS = D // P
 C_BLOCKS = C // P
+
+WARM_MATMULS = 5
 
 FLOPS = 2 * 2 * D * C * N
 
@@ -26,6 +29,12 @@ def tile_loraexplicitgrucell_kernel(tc, base, x, carry, w_u, b_u, w_c, b_c, offs
         nc.gpsimd.memset(warm[:], 0.0)
         nc.scalar.activation(warm[:], warm[:], SIGMOID)
 
+        zeros = held.tile([P, N], BF16, name="zeros")
+        nc.vector.memset(zeros[:], 0.0)
+        unused = psum.tile([P, N], F32, name="unused", bufs=1)
+        for i in range(WARM_MATMULS):
+            nc.tensor.matmul(unused[:], zeros[:, 0:P], zeros[:], start=True, stop=True)
+
         x_sb = held.tile([P, D_BLOCKS, N], BF16, name="x_sb")
         nc.sync.dma_start(x_sb[:], x.rearrange("(p k) n -> p k n", k=D_BLOCKS))
         w_c_sb = held.tile([P, D_BLOCKS, C], BF16, name="w_c_sb")
@@ -39,23 +48,25 @@ def tile_loraexplicitgrucell_kernel(tc, base, x, carry, w_u, b_u, w_c, b_c, offs
         offsets = held.tile([P, N // 16], U16, name="offsets")
         nc.sync.dma_start(offsets[:], offs)
 
-        carries = []
-        windows = []
+        carries = [held.tile([P, N], F32, name=f"carry{b}") for b in range(C_BLOCKS)]
+        windows = [held.tile([P, S], F32, name=f"window{b}") for b in range(C_BLOCKS)]
         for b in range(C_BLOCKS):
-            carry_sb = held.tile([P, N], F32, name=f"carry{b}")
-            nc.sync.dma_start(carry_sb[:], carry_blocks[b])
-            carries.append(carry_sb)
-            window = held.tile([P, S], F32, name=f"window{b}")
-            nc.sync.dma_start(window[:], base_blocks[b])
-            windows.append(window)
+            nc.sync.dma_start(carries[b][:], carry_blocks[b])
+            nc.sync.dma_start(windows[b][:], base_blocks[b])
 
         w_c_blocks = w_c_sb[:].rearrange("p k (m b) -> p k b m", b=C_BLOCKS)
         w_u_blocks = w_u_sb[:].rearrange("p k (m b) -> p k b m", b=C_BLOCKS)
 
         cands = [held.tile([P, N], F32, name=f"cand{b}") for b in range(C_BLOCKS)]
         us = [held.tile([P, N], F32, name=f"u{b}") for b in range(C_BLOCKS)]
-        diffs = [held.tile([P, N], F32, name=f"diff{b}") for b in range(C_BLOCKS)]
+        diffs = [held.tile([P, N], F32, name="diff0")]
+        diffs += [psum.tile([P, N], F32, name=f"diff{b}", bufs=1) for b in range(1, C_BLOCKS)]
         gateds = [held.tile([P, N], F32, name=f"gated{b}") for b in range(C_BLOCKS)]
+
+        plus = held.tile([P, P], F32, name="plus")
+        make_identity(nc, plus[:])
+        minus = held.tile([P, P], F32, name="minus")
+        nc.vector.tensor_scalar_mul(minus[:], plus[:], -1.0)
 
         for b in range(C_BLOCKS):
             z_c = psum.tile([P, N], F32, name="z_c")
@@ -67,11 +78,12 @@ def tile_loraexplicitgrucell_kernel(tc, base, x, carry, w_u, b_u, w_c, b_c, offs
                     )
             nc.scalar.activation(cands[b][:], z_c[:], TANH, bias=b_c_sb[:, b : b + 1])
             nc.scalar.activation(us[b][:], z_u[:], SIGMOID, bias=b_u_sb[:, b : b + 1])
+            if b > 0:
+                nc.tensor.matmul(diffs[b][:], plus[:], carries[b][:], start=True, stop=False)
+                nc.tensor.matmul(diffs[b][:], minus[:], cands[b][:], start=False, stop=True)
 
         nc.vector.tensor_tensor(diffs[0][:], carries[0][:], cands[0][:], SUBTRACT)
         for b in range(C_BLOCKS):
             nc.vector.tensor_tensor(gateds[b][:], us[b][:], diffs[b][:], MULT)
-            if b + 1 < C_BLOCKS:
-                nc.vector.tensor_tensor(diffs[b + 1][:], carries[b + 1][:], cands[b + 1][:], SUBTRACT)
             nc.vector.tensor_tensor(windows[b][:].indirect(offsets[:]), gateds[b][:], cands[b][:], ADD)
             nc.sync.dma_start(out_blocks[b], windows[b][:])

@@ -5,6 +5,7 @@ P = 128
 D, C, S, N = 256, 512, 2048, 512
 D_BLOCKS = D // P
 C_BLOCKS = C // P
+HALF = C // 2
 
 WARM_MATMULS = 5
 
@@ -17,9 +18,11 @@ SIGMOID, TANH = mybir.ActivationFunctionType.Sigmoid, mybir.ActivationFunctionTy
 
 def tile_loraexplicitgrucell_kernel(tc, base, x, carry, w_u, b_u, w_c, b_c, offs, out):
     nc = tc.nc
-    base_blocks = base.rearrange("(p b) s -> b p s", b=C_BLOCKS)
-    carry_blocks = carry.rearrange("(p b) n -> b p n", b=C_BLOCKS)
-    out_blocks = out.rearrange("(p b) s -> b p s", b=C_BLOCKS)
+    base_blocks = base.rearrange("(b p) s -> b p s", p=P)
+    carry_blocks = carry.rearrange("(b p) n -> b p n", p=P)
+    out_blocks = out.rearrange("(b p) s -> b p s", p=P)
+    w_c_rows = w_c.rearrange("(p k) c -> p k c", k=D_BLOCKS)
+    w_u_rows = w_u.rearrange("(p k) c -> p k c", k=D_BLOCKS)
 
     with (
         tc.tile_pool(name="held", bufs=1) as held,
@@ -36,26 +39,27 @@ def tile_loraexplicitgrucell_kernel(tc, base, x, carry, w_u, b_u, w_c, b_c, offs
             nc.tensor.matmul(unused[:], zeros[:, 0:P], zeros[:], start=True, stop=True)
 
         x_sb = held.tile([P, D_BLOCKS, N], BF16, name="x_sb")
-        nc.sync.dma_start(x_sb[:], x.rearrange("(p k) n -> p k n", k=D_BLOCKS))
-        w_c_sb = held.tile([P, D_BLOCKS, C], BF16, name="w_c_sb")
-        nc.sync.dma_start(w_c_sb[:], w_c.rearrange("(p k) c -> p k c", k=D_BLOCKS))
+        w_c_halves = [held.tile([P, D_BLOCKS, HALF], BF16, name=f"w_c_half{h}") for h in range(2)]
+        w_u_halves = [held.tile([P, D_BLOCKS, HALF], BF16, name=f"w_u_half{h}") for h in range(2)]
         b_c_sb = held.tile([P, C_BLOCKS], F32, name="b_c_sb")
-        nc.sync.dma_start(b_c_sb[:], b_c.rearrange("(p b) o -> p (b o)", b=C_BLOCKS))
-        w_u_sb = held.tile([P, D_BLOCKS, C], BF16, name="w_u_sb")
-        nc.sync.dma_start(w_u_sb[:], w_u.rearrange("(p k) c -> p k c", k=D_BLOCKS))
         b_u_sb = held.tile([P, C_BLOCKS], F32, name="b_u_sb")
-        nc.sync.dma_start(b_u_sb[:], b_u.rearrange("(p b) o -> p (b o)", b=C_BLOCKS))
         offsets = held.tile([P, N // 16], U16, name="offsets")
-        nc.sync.dma_start(offsets[:], offs)
-
         carries = [held.tile([P, N], F32, name=f"carry{b}") for b in range(C_BLOCKS)]
         windows = [held.tile([P, S], F32, name=f"window{b}") for b in range(C_BLOCKS)]
-        for b in range(C_BLOCKS):
+
+        nc.sync.dma_start(x_sb[:], x.rearrange("(p k) n -> p k n", k=D_BLOCKS))
+        nc.sync.dma_start(w_c_halves[0][:], w_c_rows[:, :, 0:HALF])
+        nc.sync.dma_start(b_c_sb[:], b_c.rearrange("(b p) o -> p (b o)", p=P))
+        nc.sync.dma_start(w_u_halves[0][:], w_u_rows[:, :, 0:HALF])
+        nc.sync.dma_start(b_u_sb[:], b_u.rearrange("(b p) o -> p (b o)", p=P))
+        nc.sync.dma_start(offsets[:], offs)
+        nc.sync.dma_start(carries[0][:], carry_blocks[0])
+        nc.sync.dma_start(windows[0][:], base_blocks[0])
+        nc.sync.dma_start(w_c_halves[1][:], w_c_rows[:, :, HALF:C])
+        nc.sync.dma_start(w_u_halves[1][:], w_u_rows[:, :, HALF:C])
+        for b in range(1, C_BLOCKS):
             nc.sync.dma_start(carries[b][:], carry_blocks[b])
             nc.sync.dma_start(windows[b][:], base_blocks[b])
-
-        w_c_blocks = w_c_sb[:].rearrange("p k (m b) -> p k b m", b=C_BLOCKS)
-        w_u_blocks = w_u_sb[:].rearrange("p k (m b) -> p k b m", b=C_BLOCKS)
 
         cands = [held.tile([P, N], F32, name=f"cand{b}") for b in range(C_BLOCKS)]
         us = [held.tile([P, N], F32, name=f"u{b}") for b in range(C_BLOCKS)]
@@ -71,10 +75,11 @@ def tile_loraexplicitgrucell_kernel(tc, base, x, carry, w_u, b_u, w_c, b_c, offs
         for b in range(C_BLOCKS):
             z_c = psum.tile([P, N], F32, name="z_c")
             z_u = psum.tile([P, N], F32, name="z_u")
-            for z, w_blocks in ((z_c, w_c_blocks), (z_u, w_u_blocks)):
+            columns = slice((b % 2) * P, (b % 2 + 1) * P)
+            for z, w_halves in ((z_c, w_c_halves), (z_u, w_u_halves)):
                 for k in range(D_BLOCKS):
                     nc.tensor.matmul(
-                        z[:], w_blocks[:, k, b, :], x_sb[:, k, :], start=(k == 0), stop=(k == D_BLOCKS - 1)
+                        z[:], w_halves[b // 2][:, k, columns], x_sb[:, k, :], start=(k == 0), stop=(k == D_BLOCKS - 1)
                     )
             nc.scalar.activation(cands[b][:], z_c[:], TANH, bias=b_c_sb[:, b : b + 1])
             nc.scalar.activation(us[b][:], z_u[:], SIGMOID, bias=b_u_sb[:, b : b + 1])

@@ -7,7 +7,7 @@ D_BLOCKS = D // P
 C_BLOCKS = C // P
 HALF = C // 2
 
-WARM_MATMULS = 5
+WARM_MATMULS = 4
 
 FLOPS = 2 * 2 * D * C * N
 
@@ -55,9 +55,11 @@ def tile_loraexplicitgrucell_kernel(tc, base, x, carry, w_u, b_u, w_c, b_c, offs
         nc.sync.dma_start(offsets[:], offs)
         nc.sync.dma_start(carries[0][:], carry_blocks[0])
         nc.sync.dma_start(windows[0][:], base_blocks[0])
+        nc.sync.dma_start(carries[1][:], carry_blocks[1])
         nc.sync.dma_start(w_c_halves[1][:], w_c_rows[:, :, HALF:C])
         nc.sync.dma_start(w_u_halves[1][:], w_u_rows[:, :, HALF:C])
-        for b in range(1, C_BLOCKS):
+        nc.sync.dma_start(windows[1][:], base_blocks[1])
+        for b in range(2, C_BLOCKS):
             nc.sync.dma_start(carries[b][:], carry_blocks[b])
             nc.sync.dma_start(windows[b][:], base_blocks[b])
 
@@ -70,7 +72,7 @@ def tile_loraexplicitgrucell_kernel(tc, base, x, carry, w_u, b_u, w_c, b_c, offs
         plus = held.tile([P, P], F32, name="plus")
         make_identity(nc, plus[:])
         minus = held.tile([P, P], F32, name="minus")
-        nc.vector.tensor_scalar_mul(minus[:], plus[:], -1.0)
+        nc.gpsimd.tensor_scalar_mul(minus[:], plus[:], -1.0)
 
         for b in range(C_BLOCKS):
             z_c = psum.tile([P, N], F32, name="z_c")

@@ -6,6 +6,7 @@ D, C, S, N = 256, 512, 2048, 512
 D_BLOCKS = D // P
 C_BLOCKS = C // P
 HALF = C // 2
+PAD = 8
 
 WARM_MATMULS = 4
 
@@ -18,9 +19,12 @@ SIGMOID, TANH = mybir.ActivationFunctionType.Sigmoid, mybir.ActivationFunctionTy
 
 def tile_loraexplicitgrucell_kernel(tc, base, x, carry, w_u, b_u, w_c, b_c, offs, out):
     nc = tc.nc
-    base_blocks = base.rearrange("(b p) s -> b p s", p=P)
-    carry_blocks = carry.rearrange("(b p) n -> b p n", p=P)
-    out_blocks = out.rearrange("(b p) s -> b p s", p=P)
+    base_views = base.rearrange("(h p i) s -> h i p s", h=2, i=2)
+    carry_views = carry.rearrange("(h p i) n -> h i p n", h=2, i=2)
+    out_views = out.rearrange("(h p i) s -> h i p s", h=2, i=2)
+    base_blocks = [base_views[b // 2, b % 2] for b in range(C_BLOCKS)]
+    carry_blocks = [carry_views[b // 2, b % 2] for b in range(C_BLOCKS)]
+    out_blocks = [out_views[b // 2, b % 2] for b in range(C_BLOCKS)]
     w_c_rows = w_c.rearrange("(p k) c -> p k c", k=D_BLOCKS)
     w_u_rows = w_u.rearrange("(p k) c -> p k c", k=D_BLOCKS)
 
@@ -41,17 +45,17 @@ def tile_loraexplicitgrucell_kernel(tc, base, x, carry, w_u, b_u, w_c, b_c, offs
         x_sb = held.tile([P, D_BLOCKS, N], BF16, name="x_sb")
         w_c_halves = [held.tile([P, D_BLOCKS, HALF], BF16, name=f"w_c_half{h}") for h in range(2)]
         w_u_halves = [held.tile([P, D_BLOCKS, HALF], BF16, name=f"w_u_half{h}") for h in range(2)]
-        b_c_sb = held.tile([P, C_BLOCKS], F32, name="b_c_sb")
-        b_u_sb = held.tile([P, C_BLOCKS], F32, name="b_u_sb")
+        b_c_sb = held.tile([P, 2, PAD], F32, name="b_c_sb")
+        b_u_sb = held.tile([P, 2, PAD], F32, name="b_u_sb")
         offsets = held.tile([P, N // 16], U16, name="offsets")
         carries = [held.tile([P, N], F32, name=f"carry{b}") for b in range(C_BLOCKS)]
         windows = [held.tile([P, S], F32, name=f"window{b}") for b in range(C_BLOCKS)]
 
         nc.sync.dma_start(x_sb[:], x.rearrange("(p k) n -> p k n", k=D_BLOCKS))
         nc.sync.dma_start(w_c_halves[0][:], w_c_rows[:, :, 0:HALF])
-        nc.sync.dma_start(b_c_sb[:], b_c.rearrange("(b p) o -> p (b o)", p=P))
+        nc.sync.dma_start(b_c_sb[:, :, 0:2], b_c.rearrange("(h p i) o -> p h (i o)", h=2, i=2))
         nc.sync.dma_start(w_u_halves[0][:], w_u_rows[:, :, 0:HALF])
-        nc.sync.dma_start(b_u_sb[:], b_u.rearrange("(b p) o -> p (b o)", p=P))
+        nc.sync.dma_start(b_u_sb[:, :, 0:2], b_u.rearrange("(h p i) o -> p h (i o)", h=2, i=2))
         nc.sync.dma_start(offsets[:], offs)
         nc.sync.dma_start(carries[0][:], carry_blocks[0])
         nc.sync.dma_start(windows[0][:], base_blocks[0])
@@ -77,17 +81,16 @@ def tile_loraexplicitgrucell_kernel(tc, base, x, carry, w_u, b_u, w_c, b_c, offs
         for b in range(C_BLOCKS):
             z_c = psum.tile([P, N], F32, name="z_c")
             z_u = psum.tile([P, N], F32, name="z_u")
-            columns = slice((b % 2) * P, (b % 2 + 1) * P)
+            h, i = divmod(b, 2)
             for z, w_halves in ((z_c, w_c_halves), (z_u, w_u_halves)):
+                w_block = w_halves[h][:].rearrange("p k (m i) -> p k i m", i=2)[:, :, i, :]
                 for k in range(D_BLOCKS):
-                    nc.tensor.matmul(
-                        z[:], w_halves[b // 2][:, k, columns], x_sb[:, k, :], start=(k == 0), stop=(k == D_BLOCKS - 1)
-                    )
-            nc.scalar.activation(cands[b][:], z_c[:], TANH, bias=b_c_sb[:, b : b + 1])
-            nc.scalar.activation(us[b][:], z_u[:], SIGMOID, bias=b_u_sb[:, b : b + 1])
+                    nc.tensor.matmul(z[:], w_block[:, k, :], x_sb[:, k, :], start=(k == 0), stop=(k == D_BLOCKS - 1))
+            nc.scalar.activation(cands[b][:], z_c[:], TANH, bias=b_c_sb[:, h, i : i + 1])
+            nc.scalar.activation(us[b][:], z_u[:], SIGMOID, bias=b_u_sb[:, h, i : i + 1])
             if b > 0:
-                nc.tensor.matmul(diffs[b][:], plus[:], carries[b][:], start=True, stop=False)
-                nc.tensor.matmul(diffs[b][:], minus[:], cands[b][:], start=False, stop=True)
+                nc.tensor.matmul(diffs[b][:], minus[:], cands[b][:], start=True, stop=False)
+                nc.tensor.matmul(diffs[b][:], plus[:], carries[b][:], start=False, stop=True)
 
         nc.vector.tensor_tensor(diffs[0][:], carries[0][:], cands[0][:], SUBTRACT)
         for b in range(C_BLOCKS):

@@ -6,7 +6,6 @@ D, C, S, N = 256, 512, 2048, 512
 D_BLOCKS = D // P
 C_BLOCKS = C // P
 HALF = C // 2
-PAD = 8
 
 WARM_MATMULS = 4
 
@@ -27,6 +26,8 @@ def tile_loraexplicitgrucell_kernel(tc, base, x, carry, w_u, b_u, w_c, b_c, offs
     out_blocks = [out_views[b // 2, b % 2] for b in range(C_BLOCKS)]
     w_c_rows = w_c.rearrange("(p k) c -> p k c", k=D_BLOCKS)
     w_u_rows = w_u.rearrange("(p k) c -> p k c", k=D_BLOCKS)
+    b_c_views = b_c.rearrange("(h p i) o -> h p (i o)", h=2, i=2)
+    b_u_views = b_u.rearrange("(h p i) o -> h p (i o)", h=2, i=2)
 
     with (
         tc.tile_pool(name="held", bufs=1) as held,
@@ -45,23 +46,25 @@ def tile_loraexplicitgrucell_kernel(tc, base, x, carry, w_u, b_u, w_c, b_c, offs
         x_sb = held.tile([P, D_BLOCKS, N], BF16, name="x_sb")
         w_c_halves = [held.tile([P, D_BLOCKS, HALF], BF16, name=f"w_c_half{h}") for h in range(2)]
         w_u_halves = [held.tile([P, D_BLOCKS, HALF], BF16, name=f"w_u_half{h}") for h in range(2)]
-        b_c_sb = held.tile([P, 2, PAD], F32, name="b_c_sb")
-        b_u_sb = held.tile([P, 2, PAD], F32, name="b_u_sb")
+        b_c_halves = [held.tile([P, 2], F32, name=f"b_c_half{h}") for h in range(2)]
+        b_u_halves = [held.tile([P, 2], F32, name=f"b_u_half{h}") for h in range(2)]
         offsets = held.tile([P, N // 16], U16, name="offsets")
         carries = [held.tile([P, N], F32, name=f"carry{b}") for b in range(C_BLOCKS)]
         windows = [held.tile([P, S], F32, name=f"window{b}") for b in range(C_BLOCKS)]
 
         nc.sync.dma_start(x_sb[:], x.rearrange("(p k) n -> p k n", k=D_BLOCKS))
         nc.sync.dma_start(w_c_halves[0][:], w_c_rows[:, :, 0:HALF])
-        nc.sync.dma_start(b_c_sb[:, :, 0:2], b_c.rearrange("(h p i) o -> p h (i o)", h=2, i=2))
+        nc.sync.dma_start(b_c_halves[0][:], b_c_views[0])
         nc.sync.dma_start(w_u_halves[0][:], w_u_rows[:, :, 0:HALF])
-        nc.sync.dma_start(b_u_sb[:, :, 0:2], b_u.rearrange("(h p i) o -> p h (i o)", h=2, i=2))
+        nc.sync.dma_start(b_u_halves[0][:], b_u_views[0])
         nc.sync.dma_start(offsets[:], offs)
         nc.sync.dma_start(carries[0][:], carry_blocks[0])
         nc.sync.dma_start(windows[0][:], base_blocks[0])
         nc.sync.dma_start(carries[1][:], carry_blocks[1])
         nc.sync.dma_start(w_c_halves[1][:], w_c_rows[:, :, HALF:C])
+        nc.sync.dma_start(b_c_halves[1][:], b_c_views[1])
         nc.sync.dma_start(w_u_halves[1][:], w_u_rows[:, :, HALF:C])
+        nc.sync.dma_start(b_u_halves[1][:], b_u_views[1])
         nc.sync.dma_start(windows[1][:], base_blocks[1])
         for b in range(2, C_BLOCKS):
             nc.sync.dma_start(carries[b][:], carry_blocks[b])
@@ -86,8 +89,8 @@ def tile_loraexplicitgrucell_kernel(tc, base, x, carry, w_u, b_u, w_c, b_c, offs
                 w_block = w_halves[h][:].rearrange("p k (m i) -> p k i m", i=2)[:, :, i, :]
                 for k in range(D_BLOCKS):
                     nc.tensor.matmul(z[:], w_block[:, k, :], x_sb[:, k, :], start=(k == 0), stop=(k == D_BLOCKS - 1))
-            nc.scalar.activation(cands[b][:], z_c[:], TANH, bias=b_c_sb[:, h, i : i + 1])
-            nc.scalar.activation(us[b][:], z_u[:], SIGMOID, bias=b_u_sb[:, h, i : i + 1])
+            nc.scalar.activation(cands[b][:], z_c[:], TANH, bias=b_c_halves[h][:, i : i + 1])
+            nc.scalar.activation(us[b][:], z_u[:], SIGMOID, bias=b_u_halves[h][:, i : i + 1])
             if b > 0:
                 nc.tensor.matmul(diffs[b][:], minus[:], cands[b][:], start=True, stop=False)
                 nc.tensor.matmul(diffs[b][:], plus[:], carries[b][:], start=False, stop=True)

import concourse.mybir as mybir
from concourse.masks import make_identity

P = 128
D, C, S, N = 256, 512, 2048, 512
D_BLOCKS = D // P
C_BLOCKS = C // P
HALF = C // 2

WARM_MATMULS = 4

FLOPS = 2 * 2 * D * C * N

F32, BF16, U16 = mybir.dt.float32, mybir.dt.bfloat16, mybir.dt.uint16
ADD, SUBTRACT, MULT = mybir.AluOpType.add, mybir.AluOpType.subtract, mybir.AluOpType.mult
SIGMOID, TANH = mybir.ActivationFunctionType.Sigmoid, mybir.ActivationFunctionType.Tanh


def tile_loraexplicitgrucell_kernel(tc, base, x, carry, w_u, b_u, w_c, b_c, offs, out):
    nc = tc.nc
    base_views = base.rearrange("(h p i) s -> h i p s", h=2, i=2)
    carry_views = carry.rearrange("(h p i) n -> h i p n", h=2, i=2)
    out_views = out.rearrange("(h p i) s -> h i p s", h=2, i=2)
    base_blocks = [base_views[b // 2, b % 2] for b in range(C_BLOCKS)]
    carry_blocks = [carry_views[b // 2, b % 2] for b in range(C_BLOCKS)]
    out_blocks = [out_views[b // 2, b % 2] for b in range(C_BLOCKS)]
    w_c_rows = w_c.rearrange("(p k) c -> p k c", k=D_BLOCKS)
    w_u_rows = w_u.rearrange("(p k) c -> p k c", k=D_BLOCKS)
    b_c_views = b_c.rearrange("(h p i) o -> h p (i o)", h=2, i=2)
    b_u_views = b_u.rearrange("(h p i) o -> h p (i o)", h=2, i=2)

    with (
        tc.tile_pool(name="held", bufs=1) as held,
        tc.psum_pool(name="psum", bufs=2) as psum,
    ):
        warm = held.tile([P, 1], F32, name="warm")
        nc.gpsimd.memset(warm[:], 0.0)
        nc.scalar.activation(warm[:], warm[:], SIGMOID)

        zeros = held.tile([P, N], BF16, name="zeros")
        nc.vector.memset(zeros[:], 0.0)
        unused = psum.tile([P, N], F32, name="unused", bufs=1)
        for i in range(WARM_MATMULS):
            nc.tensor.matmul(unused[:], zeros[:, 0:P], zeros[:], start=True, stop=True)

        x_sb = held.tile([P, D_BLOCKS, N], BF16, name="x_sb")
        w_c_halves = [held.tile([P, D_BLOCKS, HALF], BF16, name=f"w_c_half{h}") for h in range(2)]
        w_u_halves = [held.tile([P, D_BLOCKS, HALF], BF16, name=f"w_u_half{h}") for h in range(2)]
        b_c_halves = [held.tile([P, 2], F32, name=f"b_c_half{h}") for h in range(2)]
        b_u_halves = [held.tile([P, 2], F32, name=f"b_u_half{h}") for h in range(2)]
        offsets = held.tile([P, N // 16], U16, name="offsets")
        carries = [held.tile([P, N], F32, name=f"carry{b}") for b in range(C_BLOCKS)]
        windows = [held.tile([P, S], F32, name=f"window{b}") for b in range(C_BLOCKS)]

        nc.sync.dma_start(x_sb[:], x.rearrange("(p k) n -> p k n", k=D_BLOCKS))
        nc.sync.dma_start(w_c_halves[0][:], w_c_rows[:, :, 0:HALF])
        nc.sync.dma_start(b_c_halves[0][:], b_c_views[0])
        nc.sync.dma_start(w_u_halves[0][:], w_u_rows[:, :, 0:HALF])
        nc.sync.dma_start(b_u_halves[0][:], b_u_views[0])
        nc.sync.dma_start(offsets[:], offs)
        nc.sync.dma_start(carries[0][:], carry_blocks[0])
        nc.sync.dma_start(windows[0][:], base_blocks[0])
        nc.sync.dma_start(carries[1][:], carry_blocks[1])
        nc.sync.dma_start(w_c_halves[1][:], w_c_rows[:, :, HALF:C])
        nc.sync.dma_start(b_c_halves[1][:], b_c_views[1])
        nc.sync.dma_start(w_u_halves[1][:], w_u_rows[:, :, HALF:C])
        nc.sync.dma_start(b_u_halves[1][:], b_u_views[1])
        nc.sync.dma_start(windows[1][:], base_blocks[1])
        for b in range(2, C_BLOCKS):
            nc.sync.dma_start(carries[b][:], carry_blocks[b])
            nc.sync.dma_start(windows[b][:], base_blocks[b])

        cands = [held.tile([P, N], F32, name=f"cand{b}") for b in range(C_BLOCKS)]
        us = [held.tile([P, N], F32, name=f"u{b}") for b in range(C_BLOCKS)]
        diffs = [held.tile([P, N], F32, name="diff0")]
        diffs += [psum.tile([P, N], F32, name=f"diff{b}", bufs=1) for b in range(1, C_BLOCKS)]
        gateds = [held.tile([P, N], F32, name=f"gated{b}") for b in range(C_BLOCKS)]

        plus = held.tile([P, P], F32, name="plus")
        make_identity(nc, plus[:])
        minus = held.tile([P, P], F32, name="minus")
        nc.gpsimd.tensor_scalar_mul(minus[:], plus[:], -1.0)

        for b in range(C_BLOCKS):
            z_c = psum.tile([P, N], F32, name="z_c")
            z_u = psum.tile([P, N], F32, name="z_u")
            h, i = divmod(b, 2)
            for z, w_halves in ((z_c, w_c_halves), (z_u, w_u_halves)):
                w_block = w_halves[h][:].rearrange("p k (m i) -> p k i m", i=2)[:, :, i, :]
                for k in range(D_BLOCKS):
                    nc.tensor.matmul(z[:], w_block[:, k, :], x_sb[:, k, :], start=(k == 0), stop=(k == D_BLOCKS - 1))
            nc.scalar.activation(cands[b][:], z_c[:], TANH, bias=b_c_halves[h][:, i : i + 1])
            nc.scalar.activation(us[b][:], z_u[:], SIGMOID, bias=b_u_halves[h][:, i : i + 1])
            if b > 0:
                nc.tensor.matmul(diffs[b][:], minus[:], cands[b][:], start=True, stop=False)
                nc.tensor.matmul(diffs[b][:], plus[:], carries[b][:], start=False, stop=True)

        nc.vector.tensor_tensor(diffs[0][:], carries[0][:], cands[0][:], SUBTRACT)
        for b in range(C_BLOCKS):
            nc.vector.tensor_tensor(gateds[b][:], us[b][:], diffs[b][:], MULT)
            nc.vector.tensor_tensor(windows[b][:].indirect(offsets[:]), gateds[b][:], cands[b][:], ADD)
            nc.sync.dma_start(out_blocks[b], windows[b][:])
